import numpy as np
import ml_dtypes

BF16 = ml_dtypes.bfloat16


def bf(x):
    return np.asarray(x, np.float32).astype(BF16)


def f32(x):
    return np.asarray(x, np.float32)


def f64(x):
    return np.asarray(x).astype(np.float64)


def striped(idx):
    return np.tile(idx.reshape(-1, 16).T, (8, 1))


C, S, N, M = 128, 512, 256, 384


def setup_inputs():
    return {"emb": f32(np.random.standard_normal((C, S))), "gamma": f32(1.0 + 0.1 * np.random.standard_normal((C, 1))), "w_qkv": bf(np.random.standard_normal((C, M)) / np.sqrt(C)), "offs": striped(np.random.permutation(np.tile(np.arange(S), 2))[:N])}


def reference(emb, gamma, w_qkv, offs):
    idx = offs[:16].T.reshape(-1)
    x = f64(emb)[:, idx]
    r = np.sqrt(C) / np.sqrt(np.sum(x * x, axis=0, keepdims=True))
    y = x * r * f64(gamma)
    return np.concatenate([x, f64(w_qkv).T @ y], axis=0)

@@ -1,0 +1,83 @@
+import concourse.mybir as mybir
+
+C, S, N, M = 128, 512, 256, 384
+FLOPS = 2 * C * M * N
+
+F32, BF16, U16 = mybir.dt.float32, mybir.dt.bfloat16, mybir.dt.uint16
+MULT = mybir.AluOpType.mult
+COPY = mybir.ActivationFunctionType.Copy
+ABS_RSQRT = mybir.ActivationFunctionType.Abs_reciprocal_sqrt
+
+WIDTHS = (64, 64, 64, 64)
+assert sum(WIDTHS) == N and all(width % 32 == 0 for width in WIDTHS)
+PIECES = len(WIDTHS)
+BOUNDS = [(sum(WIDTHS[:p]), sum(WIDTHS[: p + 1])) for p in range(PIECES)]
+WIDEST = C
+assert max(WIDTHS) <= WIDEST
+STORES = 2
+H = N // STORES
+BANKS = 8
+BLOCKS = M // C
+WARM_MATMULS = 4
+
+
+def tile_ringtransformer_kernel(tc, emb, gamma, w_qkv, offs, out):
+    nc = tc.nc
+    with (
+        tc.tile_pool(name="held", bufs=1) as held,
+        tc.tile_pool(name="work", bufs=PIECES) as work,
+        tc.psum_pool(name="psum", bufs=BANKS) as psum,
+    ):
+        one = held.tile([C, 1], F32, name="one")
+        nc.vector.memset(one[:], 1.0)
+        warmed = held.tile([C, 1], F32, name="warmed")
+        nc.scalar.activation(warmed[:], one[:], ABS_RSQRT)
+
+        offsets = held.tile([C, N // 16], U16, name="offsets")
+        nc.sync.dma_start(offsets[:], offs)
+        table = held.tile([C, S], F32, name="table")
+        nc.sync.dma_start(table[:], emb)
+        weights = held.tile([C, M], BF16, name="weights")
+        nc.sync.dma_start(weights[:], w_qkv)
+        gain = held.tile([C, 1], F32, name="gain")
+        nc.sync.dma_start(gain[:], gamma)
+
+        averager = held.tile([C, C], F32, name="averager")
+        nc.vector.memset(averager[:], 1.0 / C)
+
+        idle_product = psum.tile([C, WIDEST], F32, name="bank")
+        for i in range(WARM_MATMULS):
+            nc.tensor.matmul(idle_product[:, 0:C], averager[:], averager[:], start=True, stop=True)
+
+
+        x = held.tile([C, N], F32, name="x")
+        for lo, hi in BOUNDS:
+            nc.scalar.activation(x[:, lo:hi], table[:].indirect(offsets[:, lo // 16 : hi // 16]), COPY)
+        for s in range(STORES):
+            nc.sync.dma_start(out[0:C, s * H : (s + 1) * H], x[:, s * H : (s + 1) * H])
+
+        mean_square = []
+        for lo, hi in BOUNDS:
+            squares = work.tile([C, WIDEST], F32, name="squares")
+            nc.vector.tensor_tensor(squares[:, 0 : hi - lo], x[:, lo:hi], x[:, lo:hi], MULT)
+            mean_square.append(psum.tile([C, WIDEST], F32, name="bank"))
+            nc.tensor.matmul(mean_square[-1][:, 0 : hi - lo], averager[:], squares[:, 0 : hi - lo], start=True, stop=True)
+
+        y = held.tile([C, N], BF16, name="y")
+        for p, (lo, hi) in enumerate(BOUNDS):
+            r = work.tile([C, WIDEST], F32, name="r")
+            nc.scalar.activation(r[:, 0 : hi - lo], mean_square[p][:, 0 : hi - lo], ABS_RSQRT)
+            nc.vector.scalar_tensor_tensor(y[:, lo:hi], x[:, lo:hi], gain[:, 0:1], r[:, 0 : hi - lo], MULT, MULT)
+
+        staged = held.tile([C, BLOCKS, N], F32, name="staged")
+        for p, (lo, hi) in enumerate(BOUNDS):
+            for b in range(BLOCKS):
+                product = psum.tile([C, WIDEST], F32, name="bank")
+                nc.tensor.matmul(product[:, 0 : hi - lo], weights[:, b * C : (b + 1) * C], y[:, lo:hi], start=True, stop=True)
+                if (p * BLOCKS + b) % 2 == 0:
+                    nc.vector.tensor_copy(staged[:, b, lo:hi], product[:, 0 : hi - lo])
+                else:
+                    nc.scalar.copy(staged[:, b, lo:hi], product[:, 0 : hi - lo])
+        projected = out[C:, :].rearrange("(b c) j -> c b j", c=C)
+        for s in range(STORES):
+            nc.sync.dma_start(projected[:, :, s * H : (s + 1) * H], staged[:, :, s * H : (s + 1) * H])

@@ -16,6 +16,7 @@ WIDEST = C
 assert max(WIDTHS) <= WIDEST
 STORES = 2
 H = N // STORES
+DMA_ALIGN = 256
 BANKS = 8
 BLOCKS = M // C
 WARM_MATMULS = 4
@@ -35,9 +36,9 @@ def tile_ringtransformer_kernel(tc, emb, gamma, w_qkv, offs, out):
 
         offsets = held.tile([C, N // 16], U16, name="offsets")
         nc.sync.dma_start(offsets[:], offs)
-        table = held.tile([C, S], F32, name="table")
+        table = held.tile([C, S], F32, name="table", align_bytes=DMA_ALIGN)
         nc.sync.dma_start(table[:], emb)
-        weights = held.tile([C, M], BF16, name="weights")
+        weights = held.tile([C, M], BF16, name="weights", align_bytes=DMA_ALIGN)
         nc.sync.dma_start(weights[:], w_qkv)
         gain = held.tile([C, 1], F32, name="gain")
         nc.sync.dma_start(gain[:], gamma)
@@ -50,7 +51,7 @@ def tile_ringtransformer_kernel(tc, emb, gamma, w_qkv, offs, out):
             nc.tensor.matmul(idle_product[:, 0:C], averager[:], averager[:], start=True, stop=True)
 
 
-        x = held.tile([C, N], F32, name="x")
+        x = held.tile([C, N], F32, name="x", align_bytes=DMA_ALIGN)
         for lo, hi in BOUNDS:
             nc.scalar.activation(x[:, lo:hi], table[:].indirect(offsets[:, lo // 16 : hi // 16]), COPY)
         for s in range(STORES):
@@ -69,7 +70,7 @@ def tile_ringtransformer_kernel(tc, emb, gamma, w_qkv, offs, out):
             nc.scalar.activation(r[:, 0 : hi - lo], mean_square[p][:, 0 : hi - lo], ABS_RSQRT)
             nc.vector.scalar_tensor_tensor(y[:, lo:hi], x[:, lo:hi], gain[:, 0:1], r[:, 0 : hi - lo], MULT, MULT)
 
-        staged = held.tile([C, BLOCKS, N], F32, name="staged")
+        staged = held.tile([C, BLOCKS, N], F32, name="staged", align_bytes=DMA_ALIGN)
         for p, (lo, hi) in enumerate(BOUNDS):
             for b in range(BLOCKS):
                 product = psum.tile([C, WIDEST], F32, name="bank")

@@ -34,10 +34,10 @@ def tile_ringtransformer_kernel(tc, emb, gamma, w_qkv, offs, out):
         warmed = held.tile([C, 1], F32, name="warmed")
         nc.scalar.activation(warmed[:], one[:], ABS_RSQRT)
 
-        offsets = held.tile([C, N // 16], U16, name="offsets")
-        nc.sync.dma_start(offsets[:], offs)
         table = held.tile([C, S], F32, name="table", align_bytes=DMA_ALIGN)
         nc.sync.dma_start(table[:], emb)
+        offsets = held.tile([C, N // 16], U16, name="offsets")
+        nc.sync.dma_start(offsets[:], offs)
         weights = held.tile([C, M], BF16, name="weights", align_bytes=DMA_ALIGN)
         nc.sync.dma_start(weights[:], w_qkv)
         gain = held.tile([C, 1], F32, name="gain")

@@ -29,22 +29,20 @@ def tile_ringtransformer_kernel(tc, emb, gamma, w_qkv, offs, out):
         tc.tile_pool(name="work", bufs=PIECES) as work,
         tc.psum_pool(name="psum", bufs=BANKS) as psum,
     ):
-        one = held.tile([C, 1], F32, name="one")
-        nc.vector.memset(one[:], 1.0)
+        averager = held.tile([C, C], F32, name="averager")
+        nc.vector.memset(averager[:], 1.0 / C)
+
         warmed = held.tile([C, 1], F32, name="warmed")
-        nc.scalar.activation(warmed[:], one[:], ABS_RSQRT)
+        nc.scalar.activation(warmed[:], averager[:, 0:1], ABS_RSQRT)
 
         table = held.tile([C, S], F32, name="table", align_bytes=DMA_ALIGN)
         nc.sync.dma_start(table[:], emb)
-        offsets = held.tile([C, N // 16], U16, name="offsets")
+        offsets = held.tile([C, N // 16], U16, name="offsets", align_bytes=DMA_ALIGN)
         nc.sync.dma_start(offsets[:], offs)
         weights = held.tile([C, M], BF16, name="weights", align_bytes=DMA_ALIGN)
         nc.sync.dma_start(weights[:], w_qkv)
         gain = held.tile([C, 1], F32, name="gain")
         nc.sync.dma_start(gain[:], gamma)
-
-        averager = held.tile([C, C], F32, name="averager")
-        nc.vector.memset(averager[:], 1.0 / C)
 
         idle_product = psum.tile([C, WIDEST], F32, name="bank")
         for i in range(WARM_MATMULS):

import concourse.mybir as mybir

C, S, N, M = 128, 512, 256, 384
FLOPS = 2 * C * M * N

F32, BF16, U16 = mybir.dt.float32, mybir.dt.bfloat16, mybir.dt.uint16
MULT = mybir.AluOpType.mult
COPY = mybir.ActivationFunctionType.Copy
ABS_RSQRT = mybir.ActivationFunctionType.Abs_reciprocal_sqrt

WIDTHS = (64, 64, 64, 64)
assert sum(WIDTHS) == N and all(width % 32 == 0 for width in WIDTHS)
PIECES = len(WIDTHS)
BOUNDS = [(sum(WIDTHS[:p]), sum(WIDTHS[: p + 1])) for p in range(PIECES)]
WIDEST = C
assert max(WIDTHS) <= WIDEST
STORES = 2
H = N // STORES
DMA_ALIGN = 256
BANKS = 8
BLOCKS = M // C
WARM_MATMULS = 4


def tile_ringtransformer_kernel(tc, emb, gamma, w_qkv, offs, out):
    nc = tc.nc
    with (
        tc.tile_pool(name="held", bufs=1) as held,
        tc.tile_pool(name="work", bufs=PIECES) as work,
        tc.psum_pool(name="psum", bufs=BANKS) as psum,
    ):
        averager = held.tile([C, C], F32, name="averager")
        nc.vector.memset(averager[:], 1.0 / C)

        warmed = held.tile([C, 1], F32, name="warmed")
        nc.scalar.activation(warmed[:], averager[:, 0:1], ABS_RSQRT)

        table = held.tile([C, S], F32, name="table", align_bytes=DMA_ALIGN)
        nc.sync.dma_start(table[:], emb)
        offsets = held.tile([C, N // 16], U16, name="offsets", align_bytes=DMA_ALIGN)
        nc.sync.dma_start(offsets[:], offs)
        weights = held.tile([C, M], BF16, name="weights", align_bytes=DMA_ALIGN)
        nc.sync.dma_start(weights[:], w_qkv)
        gain = held.tile([C, 1], F32, name="gain")
        nc.sync.dma_start(gain[:], gamma)

        idle_product = psum.tile([C, WIDEST], F32, name="bank")
        for i in range(WARM_MATMULS):
            nc.tensor.matmul(idle_product[:, 0:C], averager[:], averager[:], start=True, stop=True)


        x = held.tile([C, N], F32, name="x", align_bytes=DMA_ALIGN)
        for lo, hi in BOUNDS:
            nc.scalar.activation(x[:, lo:hi], table[:].indirect(offsets[:, lo // 16 : hi // 16]), COPY)
        for s in range(STORES):
            nc.sync.dma_start(out[0:C, s * H : (s + 1) * H], x[:, s * H : (s + 1) * H])

        mean_square = []
        for lo, hi in BOUNDS:
            squares = work.tile([C, WIDEST], F32, name="squares")
            nc.vector.tensor_tensor(squares[:, 0 : hi - lo], x[:, lo:hi], x[:, lo:hi], MULT)
            mean_square.append(psum.tile([C, WIDEST], F32, name="bank"))
            nc.tensor.matmul(mean_square[-1][:, 0 : hi - lo], averager[:], squares[:, 0 : hi - lo], start=True, stop=True)

        y = held.tile([C, N], BF16, name="y")
        for p, (lo, hi) in enumerate(BOUNDS):
            r = work.tile([C, WIDEST], F32, name="r")
            nc.scalar.activation(r[:, 0 : hi - lo], mean_square[p][:, 0 : hi - lo], ABS_RSQRT)
            nc.vector.scalar_tensor_tensor(y[:, lo:hi], x[:, lo:hi], gain[:, 0:1], r[:, 0 : hi - lo], MULT, MULT)

        staged = held.tile([C, BLOCKS, N], F32, name="staged", align_bytes=DMA_ALIGN)
        for p, (lo, hi) in enumerate(BOUNDS):
            for b in range(BLOCKS):
                product = psum.tile([C, WIDEST], F32, name="bank")
                nc.tensor.matmul(product[:, 0 : hi - lo], weights[:, b * C : (b + 1) * C], y[:, lo:hi], start=True, stop=True)
                if (p * BLOCKS + b) % 2 == 0:
                    nc.vector.tensor_copy(staged[:, b, lo:hi], product[:, 0 : hi - lo])
                else:
                    nc.scalar.copy(staged[:, b, lo:hi], product[:, 0 : hi - lo])
        projected = out[C:, :].rearrange("(b c) j -> c b j", c=C)
        for s in range(STORES):
            nc.sync.dma_start(projected[:, :, s * H : (s + 1) * H], staged[:, :, s * H : (s + 1) * H])
